import numpy as np
import ml_dtypes


def mxq(x, axis, fmt="e4m3"):
    dtype, down = {"e4m3": (ml_dtypes.float8_e4m3fn, 7), "e5m2": (ml_dtypes.float8_e5m2, 14)}[fmt]
    v = np.moveaxis(np.asarray(x, np.float32).astype(ml_dtypes.bfloat16).astype(np.float64), axis, -1)
    blocks = v.reshape(v.shape[:-1] + (-1, 32))
    amax = np.abs(blocks).max(-1, keepdims=True)
    byte = np.maximum(np.where(amax > 0, np.frexp(amax)[1] - 1 + 127, 0) - down, 1)
    scale = np.exp2(byte - 127.0)
    codes = (blocks / scale).astype(np.float32).astype(dtype).astype(np.float64)
    return np.moveaxis((codes * scale).reshape(v.shape), -1, axis)


WIDE = False


def mx_kscale(k):
    if not WIDE:
        return np.ones(k)
    levels = np.array([20, -20, 10, -10, 0])
    a = np.random.permutation(np.resize(levels, k // 512 * 4)).reshape(k // 512, 4)
    idx = np.arange(k)
    return np.exp2(a[idx // 512, idx % 128 // 32])


BF16 = ml_dtypes.bfloat16


def bf(x):
    return np.asarray(x, np.float32).astype(BF16)


def f64(x):
    return np.asarray(x).astype(np.float64)


N, MI, MO, LMAX = 512, 512, 512, 3
C = (LMAX + 1) ** 2


def setup_inputs():
    u = mx_kscale(MO)
    d = {"x": bf(np.random.standard_normal((N, MI, C)))}
    for l in range(LMAX + 1):
        d["w%d" % l] = bf(np.random.standard_normal((MI, MO)) / np.sqrt(MI) / u[None, :])
    g = np.random.standard_normal((N, MO, C)) * np.exp2(np.random.randint(-12, 1, (N, 1, 1))) * 4.0 * u[None, :, None]
    d["grad_out"] = bf(g)
    return d


def reference(x, w0, w1, w2, w3, grad_out):
    gq = mxq(f64(grad_out), 1, "e5m2")
    parts = []
    for l, w in enumerate([w0, w1, w2, w3]):
        gl = gq[:, :, l * l:(l + 1) ** 2].transpose(0, 2, 1)
        parts.append((gl @ mxq(f64(w), 1, "e4m3").T).transpose(0, 2, 1))
    return np.concatenate(parts, axis=2)

@@ -1,0 +1,181 @@
+from contextlib import ExitStack
+
+import concourse.mybir as mybir
+from concourse.masks import make_identity
+
+F32 = mybir.dt.float32
+BF16 = mybir.dt.bfloat16
+U32 = mybir.dt.uint32
+U8 = mybir.dt.uint8
+E4M3X4 = mybir.dt.float8_e4m3fn_x4
+E5M2X4 = mybir.dt.float8_e5m2_x4
+
+P = 128
+N = 512
+MI = 512
+MO = 512
+C = 16
+NB = N // P
+QUADS = C // 4
+
+FLOPS = 2 * N * MI * MO * C
+BYTES = N * MO * C * 2 + 4 * MI * MO * 2 + N * MI * C * 4
+
+
+def degree(c):
+    return 0 if c < 1 else 1 if c < 4 else 2 if c < 9 else 3
+
+
+def tile_irrepsstridelinear_t_kernel(tc, x, w0, w1, w2, w3, grad_out, out):
+    nc = tc.nc
+    weights = [w0, w1, w2, w3]
+    with ExitStack() as ctx:
+        const = ctx.enter_context(tc.tile_pool(name="const", bufs=1))
+        gpool = ctx.enter_context(tc.tile_pool(name="gpool", bufs=1))
+        wpool = ctx.enter_context(tc.tile_pool(name="wpool", bufs=1))
+        wstage = ctx.enter_context(tc.tile_pool(name="wstage", bufs=2))
+        grp = ctx.enter_context(tc.tile_pool(name="grp", bufs=4))
+        qpool = ctx.enter_context(tc.tile_pool(name="qpool", bufs=4))
+        ypool = ctx.enter_context(tc.tile_pool(name="ypool", bufs=4))
+        zpool = ctx.enter_context(tc.tile_pool(name="zpool", bufs=2))
+        psum_t = ctx.enter_context(tc.psum_pool(name="psum_t", bufs=4))
+        psum_o = ctx.enter_context(tc.psum_pool(name="psum_o", bufs=4))
+
+        ident = const.tile([P, P], F32, name="ident")
+        make_identity(nc, ident[:])
+
+        g_sb = []
+        w_sb = []
+
+        def load_g(nb):
+            t = gpool.tile([P, MO * C], BF16, name="g_sb%d" % nb)
+            g_sb.append(t)
+            half = MO // 2
+            for u in range(2):
+                nc.sync.dma_start(
+                    out=t[:, u * half * C:(u + 1) * half * C],
+                    in_=grad_out[nb * P:(nb + 1) * P, u * half:(u + 1) * half, :].rearrange("n o c -> n (o c)"),
+                )
+
+        load_g(0)
+        for l in range(4):
+            t = wpool.tile([P, 4, MO], BF16, name="w_sb%d" % l)
+            w_sb.append(t)
+            nc.sync.dma_start(out=t[:], in_=weights[l].rearrange("(b p) o -> p b o", p=P))
+        for nb in range(1, NB):
+            load_g(nb)
+
+        def g_transposes(nb, q):
+            words = g_sb[nb][:].bitcast(F32).rearrange("p (u j e c) -> p u e c j", u=2, j=P, e=2, c=C // 2)
+            banks = []
+            for cpl in range(2):
+                bank = psum_t.tile([P, 4 * P], F32, name="tbank")
+                for u in range(2):
+                    for e in range(2):
+                        t = 2 * u + e
+                        nc.tensor.transpose(bank[:, t * P:(t + 1) * P], words[:, u, e, 2 * q + cpl, :], ident[:])
+                banks.append(bank)
+            return banks
+
+        def g_regroup(banks):
+            grouped = grp.tile([P, 4 * P * 4], BF16, name="grouped", align_bytes=64)
+            for cpl in range(2):
+                nc.scalar.copy(
+                    out=grouped[:, cpl * 1024:(cpl + 1) * 1024].rearrange("p (e n t) -> p e n t", e=2, n=P, t=4),
+                    in_=banks[cpl][:].bitcast(BF16).rearrange("p (t n e) -> p e n t", t=4, n=P, e=2),
+                )
+            return grouped
+
+        def g_quantise(grouped):
+            codes = qpool.tile([P, 4 * P], U32, name="g_codes", align_bytes=64)
+            scales = qpool.tile([P, 4 * P], U8, name="g_scales", align_bytes=64)
+            nc.vector.quantize_mx(out=codes[:].bitcast(E5M2X4), scales=scales[:], in_=grouped[:])
+            return codes, scales
+
+        w_codes = []
+        w_scales = []
+
+        def w_prepare(l):
+            words = w_sb[l][:].bitcast(F32)
+            grouped = wstage.tile([P, MI * 4], BF16, name="w_grouped", align_bytes=64)
+            gw = grouped[:].bitcast(F32)
+            for bp in range(2):
+                bank = psum_t.tile([P, 4 * P], F32, name="tbank")
+                for bb in range(2):
+                    for u in range(2):
+                        s = 2 * bb + u
+                        nc.tensor.transpose(bank[:, s * P:(s + 1) * P], words[:, 2 * bp + bb, u * P:(u + 1) * P], ident[:])
+                dst = gw[:, bp * 512:(bp + 1) * 512].rearrange("p (b i u) -> p b i u", b=2, i=P, u=2)
+                src = bank[:].rearrange("p (b u i) -> p b i u", b=2, u=2, i=P)
+                if bp == 0:
+                    nc.vector.tensor_copy(out=dst, in_=src)
+                else:
+                    nc.scalar.copy(out=dst, in_=src)
+            codes = wpool.tile([P, MI], U32, name="w_codes%d" % l, align_bytes=64)
+            scales = wpool.tile([P, MI], U8, name="w_scales%d" % l, align_bytes=64)
+            nc.vector.quantize_mx(out=codes[:].bitcast(E4M3X4), scales=scales[:], in_=grouped[:])
+            w_codes.append(codes)
+            w_scales.append(scales)
+
+        z_tiles = {}
+
+        def products(nb, q, codes, scales):
+            if q == 0:
+                z_tiles[nb] = zpool.tile([P, MI, C], F32, name="z")
+            z = z_tiles[nb]
+            y = ypool.tile([P, 4, MI], F32, name="y")
+            for cl in range(4):
+                l = degree(4 * q + cl)
+                acc = psum_o.tile([P, MI], F32, name="acc")
+                nc.tensor.matmul_mx(
+                    out=acc[:],
+                    lhsT=codes[:, cl * P:(cl + 1) * P].bitcast(E5M2X4),
+                    lhsT_scale=scales[:, cl * P:(cl + 1) * P],
+                    rhs=w_codes[l][:].bitcast(E4M3X4),
+                    rhs_scale=w_scales[l][:],
+                    start=True,
+                    stop=True,
+                )
+                if cl % 2 == 0:
+                    nc.vector.tensor_copy(out=y[:, cl, :], in_=acc[:])
+                else:
+                    nc.scalar.copy(out=y[:, cl, :], in_=acc[:])
+            last = nb == NB - 1 and q == QUADS - 1
+            pieces = 4 if last else 1
+            step = MI // pieces
+            for k in range(pieces):
+                nc.vector.tensor_copy(
+                    out=z[:, k * step:(k + 1) * step, 4 * q:4 * q + 4],
+                    in_=y[:, :, k * step:(k + 1) * step].rearrange("p c i -> p i c"),
+                )
+                if last:
+                    store(nb, z, k * step, (k + 1) * step)
+            if q == QUADS - 1 and not last:
+                store(nb, z, 0, MI // 2)
+                store(nb, z, MI // 2, MI)
+
+        def store(nb, z, i0, i1):
+            nc.sync.dma_start(
+                out=out[nb * P:(nb + 1) * P, i0:i1, :].rearrange("n i c -> n (i c)"),
+                in_=z[:, i0:i1, :].rearrange("p i c -> p (i c)"),
+            )
+
+        units = [(nb, q) for nb in range(NB) for q in range(QUADS)]
+        ready = {}
+
+        def prepare(k):
+            nb, q = units[k]
+            banks = g_transposes(nb, q)
+            grouped = g_regroup(banks)
+            ready[k] = g_quantise(grouped)
+
+        prepare(0)
+        prepare(1)
+        for l in range(4):
+            w_prepare(l)
+        for k in range(len(units)):
+            if k + 2 < len(units):
+                prepare(k + 2)
+            nb, q = units[k]
+            codes, scales = ready[k]
+            products(nb, q, codes, scales)

@@ -9,6 +9,8 @@ U32 = mybir.dt.uint32
 U8 = mybir.dt.uint8
 E4M3X4 = mybir.dt.float8_e4m3fn_x4
 E5M2X4 = mybir.dt.float8_e5m2_x4
+MULT = mybir.AluOpType.mult
+ADD = mybir.AluOpType.add
 
 P = 128
 N = 512
@@ -17,6 +19,9 @@ MO = 512
 C = 16
 NB = N // P
 QUADS = C // 4
+PINNED = True
+LAG = 1
+G_NUM = 6
 
 FLOPS = 2 * N * MI * MO * C
 BYTES = N * MO * C * 2 + 4 * MI * MO * 2 + N * MI * C * 4
@@ -34,12 +39,14 @@ def tile_irrepsstridelinear_t_kernel(tc, x, w0, w1, w2, w3, grad_out, out):
         gpool = ctx.enter_context(tc.tile_pool(name="gpool", bufs=1))
         wpool = ctx.enter_context(tc.tile_pool(name="wpool", bufs=1))
         wstage = ctx.enter_context(tc.tile_pool(name="wstage", bufs=2))
-        grp = ctx.enter_context(tc.tile_pool(name="grp", bufs=4))
-        qpool = ctx.enter_context(tc.tile_pool(name="qpool", bufs=4))
+        grp = ctx.enter_context(tc.tile_pool(name="grp", bufs=3))
+        qpool = ctx.enter_context(tc.tile_pool(name="qpool", bufs=6))
         ypool = ctx.enter_context(tc.tile_pool(name="ypool", bufs=4))
         zpool = ctx.enter_context(tc.tile_pool(name="zpool", bufs=2))
         psum_t = ctx.enter_context(tc.psum_pool(name="psum_t", bufs=4))
         psum_o = ctx.enter_context(tc.psum_pool(name="psum_o", bufs=4))
+        if PINNED:
+            ctx.enter_context(tc.manual_schedule())
 
         ident = const.tile([P, P], F32, name="ident")
         make_identity(nc, ident[:])
@@ -77,13 +84,15 @@ def tile_irrepsstridelinear_t_kernel(tc, x, w0, w1, w2, w3, grad_out, out):
                 banks.append(bank)
             return banks
 
-        def g_regroup(banks):
+        def g_regroup(banks, vector_helps):
             grouped = grp.tile([P, 4 * P * 4], BF16, name="grouped", align_bytes=64)
             for cpl in range(2):
-                nc.scalar.copy(
-                    out=grouped[:, cpl * 1024:(cpl + 1) * 1024].rearrange("p (e n t) -> p e n t", e=2, n=P, t=4),
-                    in_=banks[cpl][:].bitcast(BF16).rearrange("p (t n e) -> p e n t", t=4, n=P, e=2),
-                )
+                dst = grouped[:, cpl * 1024:(cpl + 1) * 1024].rearrange("p (e n t) -> p e n t", e=2, n=P, t=4)
+                src = banks[cpl][:].bitcast(BF16).rearrange("p (t n e) -> p e n t", t=4, n=P, e=2)
+                if vector_helps and cpl == 1:
+                    nc.vector.tensor_copy(out=dst, in_=src)
+                else:
+                    nc.scalar.copy(out=dst, in_=src)
             return grouped
 
         def g_quantise(grouped):
@@ -117,12 +126,13 @@ def tile_irrepsstridelinear_t_kernel(tc, x, w0, w1, w2, w3, grad_out, out):
             w_codes.append(codes)
             w_scales.append(scales)
 
-        z_tiles = {}
+        def store(nb, z, i0, i1):
+            nc.sync.dma_start(
+                out=out[nb * P:(nb + 1) * P, i0:i1, :].rearrange("n i c -> n (i c)"),
+                in_=z[:, i0:i1, :].rearrange("p i c -> p (i c)"),
+            )
 
-        def products(nb, q, codes, scales):
-            if q == 0:
-                z_tiles[nb] = zpool.tile([P, MI, C], F32, name="z")
-            z = z_tiles[nb]
+        def multiply(q, codes, scales, i0, i1):
             y = ypool.tile([P, 4, MI], F32, name="y")
             for cl in range(4):
                 l = degree(4 * q + cl)
@@ -136,46 +146,66 @@ def tile_irrepsstridelinear_t_kernel(tc, x, w0, w1, w2, w3, grad_out, out):
                     start=True,
                     stop=True,
                 )
-                if cl % 2 == 0:
-                    nc.vector.tensor_copy(out=y[:, cl, :], in_=acc[:])
+                if cl == 3 and q % 2 == 1:
+                    nc.scalar.copy(out=y[:, cl, i0:i1], in_=acc[:, i0:i1])
                 else:
-                    nc.scalar.copy(out=y[:, cl, :], in_=acc[:])
-            last = nb == NB - 1 and q == QUADS - 1
-            pieces = 4 if last else 1
-            step = MI // pieces
-            for k in range(pieces):
-                nc.vector.tensor_copy(
-                    out=z[:, k * step:(k + 1) * step, 4 * q:4 * q + 4],
-                    in_=y[:, :, k * step:(k + 1) * step].rearrange("p c i -> p i c"),
-                )
-                if last:
-                    store(nb, z, k * step, (k + 1) * step)
-            if q == QUADS - 1 and not last:
-                store(nb, z, 0, MI // 2)
-                store(nb, z, MI // 2, MI)
+                    nc.vector.tensor_copy(out=y[:, cl, i0:i1], in_=acc[:, i0:i1])
+            return y
 
-        def store(nb, z, i0, i1):
-            nc.sync.dma_start(
-                out=out[nb * P:(nb + 1) * P, i0:i1, :].rearrange("n i c -> n (i c)"),
-                in_=z[:, i0:i1, :].rearrange("p i c -> p (i c)"),
+        def interleave(z, y, q, i0, i1):
+            cut = i0 + (i1 - i0) * G_NUM // 8
+            nc.gpsimd.tensor_scalar(
+                out=z[:, i0:cut, 4 * q:4 * q + 4],
+                in0=y[:, :, i0:cut].rearrange("p c i -> p i c"),
+                scalar1=1.0,
+                scalar2=0.0,
+                op0=MULT,
+                op1=ADD,
             )
+            if cut < i1:
+                nc.scalar.copy(out=z[:, cut:i1, 4 * q:4 * q + 4], in_=y[:, :, cut:i1].rearrange("p c i -> p i c"))
 
         units = [(nb, q) for nb in range(NB) for q in range(QUADS)]
+        jobs = [(k, 0, MI) for k in range(len(units) - QUADS)]
+        for r in range(2):
+            jobs.extend([(k, r * MI // 2, (r + 1) * MI // 2) for k in range(len(units) - QUADS, len(units))])
         ready = {}
+        staged = {}
+        planes = {}
+        z_of = {}
 
-        def prepare(k):
-            nb, q = units[k]
-            banks = g_transposes(nb, q)
-            grouped = g_regroup(banks)
-            ready[k] = g_quantise(grouped)
+        def regroup(k):
+            if k < len(units):
+                nb, q = units[k]
+                staged[k] = g_regroup(g_transposes(nb, q), k < 2)
 
-        prepare(0)
-        prepare(1)
-        for l in range(4):
-            w_prepare(l)
-        for k in range(len(units)):
-            if k + 2 < len(units):
-                prepare(k + 2)
+        def quantise(k):
+            if k < len(units):
+                ready[k] = g_quantise(staged[k])
+
+        def finish(j):
+            k, i0, i1 = jobs[j]
             nb, q = units[k]
-            codes, scales = ready[k]
-            products(nb, q, codes, scales)
+            if q == 0 and i0 == 0:
+                z_of[nb] = zpool.tile([P, MI, C], F32, name="z")
+            interleave(z_of[nb], planes[j], q, i0, i1)
+            if q == QUADS - 1:
+                mid = (i0 + i1) // 2
+                store(nb, z_of[nb], i0, mid)
+                store(nb, z_of[nb], mid, i1)
+
+        regroup(0)
+        regroup(1)
+        quantise(0)
+        quantise(1)
+        for j in range(len(jobs)):
+            k, i0, i1 = jobs[j]
+            for l in range(len(w_codes), degree(4 * units[k][1] + 3) + 1):
+                w_prepare(l)
+            regroup(j + 2)
+            planes[j] = multiply(units[k][1], ready[k][0], ready[k][1], i0, i1)
+            quantise(j + 2)
+            if j >= LAG:
+                finish(j - LAG)
+        for j in range(len(jobs) - LAG, len(jobs)):
+            finish(j)

@@ -72,34 +72,45 @@ def tile_irrepsstridelinear_t_kernel(tc, x, w0, w1, w2, w3, grad_out, out):
         for nb in range(1, NB):
             load_g(nb)
 
-        def g_transposes(nb, q):
+        units = [(nb, q) for nb in range(NB) for q in range(QUADS)]
+        jobs = [(k, 0, MI) for k in range(len(units) - QUADS)]
+        for r in range(2):
+            jobs.extend([(k, r * MI // 2, (r + 1) * MI // 2) for k in range(len(units) - QUADS, len(units))])
+        ready = {}
+        staged = {}
+        planes = {}
+        z_of = {}
+
+        def g_bank(k, cpl):
+            nb, q = units[k]
             words = g_sb[nb][:].bitcast(F32).rearrange("p (u j e c) -> p u e c j", u=2, j=P, e=2, c=C // 2)
-            banks = []
-            for cpl in range(2):
-                bank = psum_t.tile([P, 4 * P], F32, name="tbank")
-                for u in range(2):
-                    for e in range(2):
-                        t = 2 * u + e
-                        nc.tensor.transpose(bank[:, t * P:(t + 1) * P], words[:, u, e, 2 * q + cpl, :], ident[:])
-                banks.append(bank)
-            return banks
+            bank = psum_t.tile([P, 4 * P], F32, name="tbank")
+            for u in range(2):
+                for e in range(2):
+                    t = 2 * u + e
+                    nc.tensor.transpose(bank[:, t * P:(t + 1) * P], words[:, u, e, 2 * q + cpl, :], ident[:])
+            return bank
 
-        def g_regroup(banks, vector_helps):
-            grouped = grp.tile([P, 4 * P * 4], BF16, name="grouped", align_bytes=64)
-            for cpl in range(2):
-                dst = grouped[:, cpl * 1024:(cpl + 1) * 1024].rearrange("p (e n t) -> p e n t", e=2, n=P, t=4)
-                src = banks[cpl][:].bitcast(BF16).rearrange("p (t n e) -> p e n t", t=4, n=P, e=2)
-                if vector_helps and cpl == 1:
-                    nc.vector.tensor_copy(out=dst, in_=src)
-                else:
-                    nc.scalar.copy(out=dst, in_=src)
-            return grouped
+        def g_regroup(k, cpl):
+            if k >= len(units):
+                return
+            if cpl == 0:
+                staged[k] = grp.tile([P, 4 * P * 4], BF16, name="grouped", align_bytes=64)
+            bank = g_bank(k, cpl)
+            dst = staged[k][:, cpl * 1024:(cpl + 1) * 1024].rearrange("p (e n t) -> p e n t", e=2, n=P, t=4)
+            src = bank[:].bitcast(BF16).rearrange("p (t n e) -> p e n t", t=4, n=P, e=2)
+            if k < 2 and cpl == 1:
+                nc.vector.tensor_copy(out=dst, in_=src)
+            else:
+                nc.scalar.copy(out=dst, in_=src)
 
-        def g_quantise(grouped):
+        def g_quantise(k):
+            if k >= len(units):
+                return
             codes = qpool.tile([P, 4 * P], U32, name="g_codes", align_bytes=64)
             scales = qpool.tile([P, 4 * P], U8, name="g_scales", align_bytes=64)
-            nc.vector.quantize_mx(out=codes[:].bitcast(E5M2X4), scales=scales[:], in_=grouped[:])
-            return codes, scales
+            nc.vector.quantize_mx(out=codes[:].bitcast(E5M2X4), scales=scales[:], in_=staged[k][:])
+            ready[k] = (codes, scales)
 
         w_codes = []
         w_scales = []
@@ -132,25 +143,27 @@ def tile_irrepsstridelinear_t_kernel(tc, x, w0, w1, w2, w3, grad_out, out):
                 in_=z[:, i0:i1, :].rearrange("p i c -> p (i c)"),
             )
 
-        def multiply(q, codes, scales, i0, i1):
-            y = ypool.tile([P, 4, MI], F32, name="y")
-            for cl in range(4):
-                l = degree(4 * q + cl)
-                acc = psum_o.tile([P, MI], F32, name="acc")
-                nc.tensor.matmul_mx(
-                    out=acc[:],
-                    lhsT=codes[:, cl * P:(cl + 1) * P].bitcast(E5M2X4),
-                    lhsT_scale=scales[:, cl * P:(cl + 1) * P],
-                    rhs=w_codes[l][:].bitcast(E4M3X4),
-                    rhs_scale=w_scales[l][:],
-                    start=True,
-                    stop=True,
-                )
-                if cl == 3 and q % 2 == 1:
-                    nc.scalar.copy(out=y[:, cl, i0:i1], in_=acc[:, i0:i1])
-                else:
-                    nc.vector.tensor_copy(out=y[:, cl, i0:i1], in_=acc[:, i0:i1])
-            return y
+        def multiply(y, k, cl, i0, i1):
+            q = units[k][1]
+            codes, scales = ready[k]
+            l = degree(4 * q + cl)
+            acc = psum_o.tile([P, MI], F32, name="acc")
+            nc.tensor.matmul_mx(
+                out=acc[:],
+                lhsT=codes[:, cl * P:(cl + 1) * P].bitcast(E5M2X4),
+                lhsT_scale=scales[:, cl * P:(cl + 1) * P],
+                rhs=w_codes[l][:].bitcast(E4M3X4),
+                rhs_scale=w_scales[l][:],
+                start=True,
+                stop=True,
+            )
+            return acc
+
+        def empty(y, acc, k, cl, i0, i1):
+            if (cl == 3 and units[k][1] % 2 == 1) or (cl % 2 == 1 and k >= len(units) - QUADS):
+                nc.scalar.copy(out=y[:, cl, i0:i1], in_=acc[:, i0:i1])
+            else:
+                nc.vector.tensor_copy(out=y[:, cl, i0:i1], in_=acc[:, i0:i1])
 
         def interleave(z, y, q, i0, i1):
             cut = i0 + (i1 - i0) * G_NUM // 8
@@ -165,24 +178,6 @@ def tile_irrepsstridelinear_t_kernel(tc, x, w0, w1, w2, w3, grad_out, out):
             if cut < i1:
                 nc.scalar.copy(out=z[:, cut:i1, 4 * q:4 * q + 4], in_=y[:, :, cut:i1].rearrange("p c i -> p i c"))
 
-        units = [(nb, q) for nb in range(NB) for q in range(QUADS)]
-        jobs = [(k, 0, MI) for k in range(len(units) - QUADS)]
-        for r in range(2):
-            jobs.extend([(k, r * MI // 2, (r + 1) * MI // 2) for k in range(len(units) - QUADS, len(units))])
-        ready = {}
-        staged = {}
-        planes = {}
-        z_of = {}
-
-        def regroup(k):
-            if k < len(units):
-                nb, q = units[k]
-                staged[k] = g_regroup(g_transposes(nb, q), k < 2)
-
-        def quantise(k):
-            if k < len(units):
-                ready[k] = g_quantise(staged[k])
-
         def finish(j):
             k, i0, i1 = jobs[j]
             nb, q = units[k]
@@ -194,17 +189,23 @@ def tile_irrepsstridelinear_t_kernel(tc, x, w0, w1, w2, w3, grad_out, out):
                 store(nb, z_of[nb], i0, mid)
                 store(nb, z_of[nb], mid, i1)
 
-        regroup(0)
-        regroup(1)
-        quantise(0)
-        quantise(1)
+        for k in range(2):
+            for cpl in range(2):
+                g_regroup(k, cpl)
+        g_quantise(0)
+        g_quantise(1)
         for j in range(len(jobs)):
             k, i0, i1 = jobs[j]
             for l in range(len(w_codes), degree(4 * units[k][1] + 3) + 1):
                 w_prepare(l)
-            regroup(j + 2)
-            planes[j] = multiply(units[k][1], ready[k][0], ready[k][1], i0, i1)
-            quantise(j + 2)
+            y = ypool.tile([P, 4, MI], F32, name="y")
+            planes[j] = y
+            for h in range(2):
+                g_regroup(j + 2, h)
+                accs = [multiply(y, k, 2 * h + d, i0, i1) for d in range(2)]
+                for d in range(2):
+                    empty(y, accs[d], k, 2 * h + d, i0, i1)
+            g_quantise(j + 2)
             if j >= LAG:
                 finish(j - LAG)
         for j in range(len(jobs) - LAG, len(jobs)):

@@ -50,6 +50,8 @@ def tile_irrepsstridelinear_t_kernel(tc, x, w0, w1, w2, w3, grad_out, out):
 
         ident = const.tile([P, P], F32, name="ident")
         make_identity(nc, ident[:])
+        ident_bf = const.tile([P, P], BF16, name="ident_bf")
+        make_identity(nc, ident_bf[:])
 
         g_sb = []
         w_sb = []
@@ -72,61 +74,46 @@ def tile_irrepsstridelinear_t_kernel(tc, x, w0, w1, w2, w3, grad_out, out):
         for nb in range(1, NB):
             load_g(nb)
 
-        units = [(nb, q) for nb in range(NB) for q in range(QUADS)]
-        jobs = [(k, 0, MI) for k in range(len(units) - QUADS)]
-        for r in range(2):
-            jobs.extend([(k, r * MI // 2, (r + 1) * MI // 2) for k in range(len(units) - QUADS, len(units))])
-        ready = {}
-        staged = {}
-        planes = {}
-        z_of = {}
+        def g_transposes(nb, q):
+            words = g_sb[nb][:].bitcast(F32).rearrange("p (t j c) -> p t c j", t=4, j=P, c=C // 2)
+            banks = []
+            for cpl in range(2):
+                bank = psum_t.tile([P, 4 * P], F32, name="tbank")
+                for t in range(4):
+                    nc.tensor.transpose(bank[:, t * P:(t + 1) * P], words[:, t, 2 * q + cpl, :], ident[:])
+                banks.append(bank)
+            return banks
 
-        def g_bank(k, cpl):
-            nb, q = units[k]
-            words = g_sb[nb][:].bitcast(F32).rearrange("p (u j e c) -> p u e c j", u=2, j=P, e=2, c=C // 2)
-            bank = psum_t.tile([P, 4 * P], F32, name="tbank")
-            for u in range(2):
-                for e in range(2):
-                    t = 2 * u + e
-                    nc.tensor.transpose(bank[:, t * P:(t + 1) * P], words[:, u, e, 2 * q + cpl, :], ident[:])
-            return bank
+        def g_regroup(banks, vector_helps):
+            grouped = grp.tile([P, 4 * P * 4], BF16, name="grouped", align_bytes=64)
+            for cpl in range(2):
+                dst = grouped[:, cpl * 1024:(cpl + 1) * 1024].rearrange("p (e n t) -> p e n t", e=2, n=P, t=4)
+                src = banks[cpl][:].bitcast(BF16).rearrange("p (t n e) -> p e n t", t=4, n=P, e=2)
+                if vector_helps and cpl == 1:
+                    nc.vector.tensor_copy(out=dst, in_=src)
+                else:
+                    nc.scalar.copy(out=dst, in_=src)
+            return grouped
 
-        def g_regroup(k, cpl):
-            if k >= len(units):
-                return
-            if cpl == 0:
-                staged[k] = grp.tile([P, 4 * P * 4], BF16, name="grouped", align_bytes=64)
-            bank = g_bank(k, cpl)
-            dst = staged[k][:, cpl * 1024:(cpl + 1) * 1024].rearrange("p (e n t) -> p e n t", e=2, n=P, t=4)
-            src = bank[:].bitcast(BF16).rearrange("p (t n e) -> p e n t", t=4, n=P, e=2)
-            if k < 2 and cpl == 1:
-                nc.vector.tensor_copy(out=dst, in_=src)
-            else:
-                nc.scalar.copy(out=dst, in_=src)
-
-        def g_quantise(k):
-            if k >= len(units):
-                return
+        def g_quantise(grouped):
             codes = qpool.tile([P, 4 * P], U32, name="g_codes", align_bytes=64)
             scales = qpool.tile([P, 4 * P], U8, name="g_scales", align_bytes=64)
-            nc.vector.quantize_mx(out=codes[:].bitcast(E5M2X4), scales=scales[:], in_=staged[k][:])
-            ready[k] = (codes, scales)
+            nc.vector.quantize_mx(out=codes[:].bitcast(E5M2X4), scales=scales[:], in_=grouped[:])
+            return codes, scales
 
         w_codes = []
         w_scales = []
 
         def w_prepare(l):
-            words = w_sb[l][:].bitcast(F32)
             grouped = wstage.tile([P, MI * 4], BF16, name="w_grouped", align_bytes=64)
-            gw = grouped[:].bitcast(F32)
             for bp in range(2):
-                bank = psum_t.tile([P, 4 * P], F32, name="tbank")
+                bank = psum_t.tile([P, 8 * P], BF16, name="tbank")
                 for bb in range(2):
-                    for u in range(2):
-                        s = 2 * bb + u
-                        nc.tensor.transpose(bank[:, s * P:(s + 1) * P], words[:, 2 * bp + bb, u * P:(u + 1) * P], ident[:])
-                dst = gw[:, bp * 512:(bp + 1) * 512].rearrange("p (b i u) -> p b i u", b=2, i=P, u=2)
-                src = bank[:].rearrange("p (b u i) -> p b i u", b=2, u=2, i=P)
+                    for t in range(4):
+                        s = 4 * bb + t
+                        nc.tensor.transpose(bank[:, s * P:(s + 1) * P], w_sb[l][:, 2 * bp + bb, t * P:(t + 1) * P], ident_bf[:])
+                dst = grouped[:, bp * 1024:(bp + 1) * 1024].rearrange("p (b i t) -> p b i t", b=2, i=P, t=4)
+                src = bank[:].rearrange("p (b t i) -> p b i t", b=2, t=4, i=P)
                 if bp == 0:
                     nc.vector.tensor_copy(out=dst, in_=src)
                 else:
@@ -143,27 +130,25 @@ def tile_irrepsstridelinear_t_kernel(tc, x, w0, w1, w2, w3, grad_out, out):
                 in_=z[:, i0:i1, :].rearrange("p i c -> p (i c)"),
             )
 
-        def multiply(y, k, cl, i0, i1):
-            q = units[k][1]
-            codes, scales = ready[k]
-            l = degree(4 * q + cl)
-            acc = psum_o.tile([P, MI], F32, name="acc")
-            nc.tensor.matmul_mx(
-                out=acc[:],
-                lhsT=codes[:, cl * P:(cl + 1) * P].bitcast(E5M2X4),
-                lhsT_scale=scales[:, cl * P:(cl + 1) * P],
-                rhs=w_codes[l][:].bitcast(E4M3X4),
-                rhs_scale=w_scales[l][:],
-                start=True,
-                stop=True,
-            )
-            return acc
-
-        def empty(y, acc, k, cl, i0, i1):
-            if (cl == 3 and units[k][1] % 2 == 1) or (cl % 2 == 1 and k >= len(units) - QUADS):
-                nc.scalar.copy(out=y[:, cl, i0:i1], in_=acc[:, i0:i1])
-            else:
-                nc.vector.tensor_copy(out=y[:, cl, i0:i1], in_=acc[:, i0:i1])
+        def multiply(q, codes, scales, i0, i1):
+            y = ypool.tile([P, 4, MI], F32, name="y")
+            for cl in range(4):
+                l = degree(4 * q + cl)
+                acc = psum_o.tile([P, MI], F32, name="acc")
+                nc.tensor.matmul_mx(
+                    out=acc[:],
+                    lhsT=codes[:, cl * P:(cl + 1) * P].bitcast(E5M2X4),
+                    lhsT_scale=scales[:, cl * P:(cl + 1) * P],
+                    rhs=w_codes[l][:].bitcast(E4M3X4),
+                    rhs_scale=w_scales[l][:],
+                    start=True,
+                    stop=True,
+                )
+                if cl == 3 and q % 2 == 1:
+                    nc.scalar.copy(out=y[:, cl, i0:i1], in_=acc[:, i0:i1])
+                else:
+                    nc.vector.tensor_copy(out=y[:, cl, i0:i1], in_=acc[:, i0:i1])
+            return y
 
         def interleave(z, y, q, i0, i1):
             cut = i0 + (i1 - i0) * G_NUM // 8
@@ -178,6 +163,24 @@ def tile_irrepsstridelinear_t_kernel(tc, x, w0, w1, w2, w3, grad_out, out):
             if cut < i1:
                 nc.scalar.copy(out=z[:, cut:i1, 4 * q:4 * q + 4], in_=y[:, :, cut:i1].rearrange("p c i -> p i c"))
 
+        units = [(nb, q) for nb in range(NB) for q in range(QUADS)]
+        jobs = [(k, 0, MI) for k in range(len(units) - QUADS)]
+        for r in range(2):
+            jobs.extend([(k, r * MI // 2, (r + 1) * MI // 2) for k in range(len(units) - QUADS, len(units))])
+        ready = {}
+        staged = {}
+        planes = {}
+        z_of = {}
+
+        def regroup(k):
+            if k < len(units):
+                nb, q = units[k]
+                staged[k] = g_regroup(g_transposes(nb, q), k < 2)
+
+        def quantise(k):
+            if k < len(units):
+                ready[k] = g_quantise(staged[k])
+
         def finish(j):
             k, i0, i1 = jobs[j]
             nb, q = units[k]
@@ -189,23 +192,17 @@ def tile_irrepsstridelinear_t_kernel(tc, x, w0, w1, w2, w3, grad_out, out):
                 store(nb, z_of[nb], i0, mid)
                 store(nb, z_of[nb], mid, i1)
 
-        for k in range(2):
-            for cpl in range(2):
-                g_regroup(k, cpl)
-        g_quantise(0)
-        g_quantise(1)
+        regroup(0)
+        regroup(1)
+        quantise(0)
+        quantise(1)
         for j in range(len(jobs)):
             k, i0, i1 = jobs[j]
             for l in range(len(w_codes), degree(4 * units[k][1] + 3) + 1):
                 w_prepare(l)
-            y = ypool.tile([P, 4, MI], F32, name="y")
-            planes[j] = y
-            for h in range(2):
-                g_regroup(j + 2, h)
-                accs = [multiply(y, k, 2 * h + d, i0, i1) for d in range(2)]
-                for d in range(2):
-                    empty(y, accs[d], k, 2 * h + d, i0, i1)
-            g_quantise(j + 2)
+            regroup(j + 2)
+            planes[j] = multiply(units[k][1], ready[k][0], ready[k][1], i0, i1)
+            quantise(j + 2)
             if j >= LAG:
                 finish(j - LAG)
         for j in range(len(jobs) - LAG, len(jobs)):

@@ -19,8 +19,8 @@ MO = 512
 C = 16
 NB = N // P
 QUADS = C // 4
-PINNED = True
-LAG = 1
+PINNED = False
+LAG = 0
 G_NUM = 6
 
 FLOPS = 2 * N * MI * MO * C
@@ -50,11 +50,9 @@ def tile_irrepsstridelinear_t_kernel(tc, x, w0, w1, w2, w3, grad_out, out):
 
         ident = const.tile([P, P], F32, name="ident")
         make_identity(nc, ident[:])
-        ident_bf = const.tile([P, P], BF16, name="ident_bf")
-        make_identity(nc, ident_bf[:])
 
         g_sb = []
-        w_sb = []
+        w_sb = {}
 
         def load_g(nb):
             t = gpool.tile([P, MO * C], BF16, name="g_sb%d" % nb)
@@ -67,20 +65,22 @@ def tile_irrepsstridelinear_t_kernel(tc, x, w0, w1, w2, w3, grad_out, out):
                 )
 
         load_g(0)
-        for l in range(4):
+        for l in reversed(range(4)):
             t = wpool.tile([P, 4, MO], BF16, name="w_sb%d" % l)
-            w_sb.append(t)
+            w_sb[l] = t
             nc.sync.dma_start(out=t[:], in_=weights[l].rearrange("(b p) o -> p b o", p=P))
         for nb in range(1, NB):
             load_g(nb)
 
         def g_transposes(nb, q):
-            words = g_sb[nb][:].bitcast(F32).rearrange("p (t j c) -> p t c j", t=4, j=P, c=C // 2)
+            words = g_sb[nb][:].bitcast(F32).rearrange("p (u j e c) -> p u e c j", u=2, j=P, e=2, c=C // 2)
             banks = []
             for cpl in range(2):
                 bank = psum_t.tile([P, 4 * P], F32, name="tbank")
-                for t in range(4):
-                    nc.tensor.transpose(bank[:, t * P:(t + 1) * P], words[:, t, 2 * q + cpl, :], ident[:])
+                for u in range(2):
+                    for e in range(2):
+                        t = 2 * u + e
+                        nc.tensor.transpose(bank[:, t * P:(t + 1) * P], words[:, u, e, 2 * q + cpl, :], ident[:])
                 banks.append(bank)
             return banks
 
@@ -101,19 +101,23 @@ def tile_irrepsstridelinear_t_kernel(tc, x, w0, w1, w2, w3, grad_out, out):
             nc.vector.quantize_mx(out=codes[:].bitcast(E5M2X4), scales=scales[:], in_=grouped[:])
             return codes, scales
 
-        w_codes = []
-        w_scales = []
+        w_codes = {}
+        w_scales = {}
 
         def w_prepare(l):
+            if l in w_codes:
+                return
+            words = w_sb[l][:].bitcast(F32)
             grouped = wstage.tile([P, MI * 4], BF16, name="w_grouped", align_bytes=64)
+            gw = grouped[:].bitcast(F32)
             for bp in range(2):
-                bank = psum_t.tile([P, 8 * P], BF16, name="tbank")
+                bank = psum_t.tile([P, 4 * P], F32, name="tbank")
                 for bb in range(2):
-                    for t in range(4):
-                        s = 4 * bb + t
-                        nc.tensor.transpose(bank[:, s * P:(s + 1) * P], w_sb[l][:, 2 * bp + bb, t * P:(t + 1) * P], ident_bf[:])
-                dst = grouped[:, bp * 1024:(bp + 1) * 1024].rearrange("p (b i t) -> p b i t", b=2, i=P, t=4)
-                src = bank[:].rearrange("p (b t i) -> p b i t", b=2, t=4, i=P)
+                    for u in range(2):
+                        s = 2 * bb + u
+                        nc.tensor.transpose(bank[:, s * P:(s + 1) * P], words[:, 2 * bp + bb, u * P:(u + 1) * P], ident[:])
+                dst = gw[:, bp * 512:(bp + 1) * 512].rearrange("p (b i u) -> p b i u", b=2, i=P, u=2)
+                src = bank[:].rearrange("p (b u i) -> p b i u", b=2, u=2, i=P)
                 if bp == 0:
                     nc.vector.tensor_copy(out=dst, in_=src)
                 else:
@@ -121,8 +125,8 @@ def tile_irrepsstridelinear_t_kernel(tc, x, w0, w1, w2, w3, grad_out, out):
             codes = wpool.tile([P, MI], U32, name="w_codes%d" % l, align_bytes=64)
             scales = wpool.tile([P, MI], U8, name="w_scales%d" % l, align_bytes=64)
             nc.vector.quantize_mx(out=codes[:].bitcast(E4M3X4), scales=scales[:], in_=grouped[:])
-            w_codes.append(codes)
-            w_scales.append(scales)
+            w_codes[l] = codes
+            w_scales[l] = scales
 
         def store(nb, z, i0, i1):
             nc.sync.dma_start(
@@ -144,7 +148,7 @@ def tile_irrepsstridelinear_t_kernel(tc, x, w0, w1, w2, w3, grad_out, out):
                     start=True,
                     stop=True,
                 )
-                if cl == 3 and q % 2 == 1:
+                if cl == 3:
                     nc.scalar.copy(out=y[:, cl, i0:i1], in_=acc[:, i0:i1])
                 else:
                     nc.vector.tensor_copy(out=y[:, cl, i0:i1], in_=acc[:, i0:i1])
@@ -161,9 +165,9 @@ def tile_irrepsstridelinear_t_kernel(tc, x, w0, w1, w2, w3, grad_out, out):
                 op1=ADD,
             )
             if cut < i1:
-                nc.scalar.copy(out=z[:, cut:i1, 4 * q:4 * q + 4], in_=y[:, :, cut:i1].rearrange("p c i -> p i c"))
+                nc.vector.tensor_copy(out=z[:, cut:i1, 4 * q:4 * q + 4], in_=y[:, :, cut:i1].rearrange("p c i -> p i c"))
 
-        units = [(nb, q) for nb in range(NB) for q in range(QUADS)]
+        units = [(nb, q) for nb in range(NB) for q in reversed(range(QUADS))]
         jobs = [(k, 0, MI) for k in range(len(units) - QUADS)]
         for r in range(2):
             jobs.extend([(k, r * MI // 2, (r + 1) * MI // 2) for k in range(len(units) - QUADS, len(units))])
@@ -184,25 +188,31 @@ def tile_irrepsstridelinear_t_kernel(tc, x, w0, w1, w2, w3, grad_out, out):
         def finish(j):
             k, i0, i1 = jobs[j]
             nb, q = units[k]
-            if q == 0 and i0 == 0:
+            if k % QUADS == 0 and i0 == 0:
                 z_of[nb] = zpool.tile([P, MI, C], F32, name="z")
             interleave(z_of[nb], planes[j], q, i0, i1)
-            if q == QUADS - 1:
+            if k % QUADS == QUADS - 1:
                 mid = (i0 + i1) // 2
                 store(nb, z_of[nb], i0, mid)
                 store(nb, z_of[nb], mid, i1)
 
+        def w_for(j):
+            if j < len(jobs):
+                q = units[jobs[j][0]][1]
+                for cl in range(4):
+                    w_prepare(degree(4 * q + cl))
+
         regroup(0)
-        regroup(1)
+        w_for(0)
         quantise(0)
+        regroup(1)
         quantise(1)
         for j in range(len(jobs)):
             k, i0, i1 = jobs[j]
-            for l in range(len(w_codes), degree(4 * units[k][1] + 3) + 1):
-                w_prepare(l)
             regroup(j + 2)
             planes[j] = multiply(units[k][1], ready[k][0], ready[k][1], i0, i1)
             quantise(j + 2)
+            w_for(j + 1)
             if j >= LAG:
                 finish(j - LAG)
         for j in range(len(jobs) - LAG, len(jobs)):

@@ -19,8 +19,8 @@ MO = 512
 C = 16
 NB = N // P
 QUADS = C // 4
-PINNED = False
-LAG = 0
+PINNED = True
+LAG = 1
 G_NUM = 6
 
 FLOPS = 2 * N * MI * MO * C
@@ -52,7 +52,7 @@ def tile_irrepsstridelinear_t_kernel(tc, x, w0, w1, w2, w3, grad_out, out):
         make_identity(nc, ident[:])
 
         g_sb = []
-        w_sb = {}
+        w_sb = []
 
         def load_g(nb):
             t = gpool.tile([P, MO * C], BF16, name="g_sb%d" % nb)
@@ -65,9 +65,9 @@ def tile_irrepsstridelinear_t_kernel(tc, x, w0, w1, w2, w3, grad_out, out):
                 )
 
         load_g(0)
-        for l in reversed(range(4)):
+        for l in range(4):
             t = wpool.tile([P, 4, MO], BF16, name="w_sb%d" % l)
-            w_sb[l] = t
+            w_sb.append(t)
             nc.sync.dma_start(out=t[:], in_=weights[l].rearrange("(b p) o -> p b o", p=P))
         for nb in range(1, NB):
             load_g(nb)
@@ -101,12 +101,10 @@ def tile_irrepsstridelinear_t_kernel(tc, x, w0, w1, w2, w3, grad_out, out):
             nc.vector.quantize_mx(out=codes[:].bitcast(E5M2X4), scales=scales[:], in_=grouped[:])
             return codes, scales
 
-        w_codes = {}
-        w_scales = {}
+        w_codes = []
+        w_scales = []
 
         def w_prepare(l):
-            if l in w_codes:
-                return
             words = w_sb[l][:].bitcast(F32)
             grouped = wstage.tile([P, MI * 4], BF16, name="w_grouped", align_bytes=64)
             gw = grouped[:].bitcast(F32)
@@ -125,8 +123,8 @@ def tile_irrepsstridelinear_t_kernel(tc, x, w0, w1, w2, w3, grad_out, out):
             codes = wpool.tile([P, MI], U32, name="w_codes%d" % l, align_bytes=64)
             scales = wpool.tile([P, MI], U8, name="w_scales%d" % l, align_bytes=64)
             nc.vector.quantize_mx(out=codes[:].bitcast(E4M3X4), scales=scales[:], in_=grouped[:])
-            w_codes[l] = codes
-            w_scales[l] = scales
+            w_codes.append(codes)
+            w_scales.append(scales)
 
         def store(nb, z, i0, i1):
             nc.sync.dma_start(
@@ -139,16 +137,17 @@ def tile_irrepsstridelinear_t_kernel(tc, x, w0, w1, w2, w3, grad_out, out):
             for cl in range(4):
                 l = degree(4 * q + cl)
                 acc = psum_o.tile([P, MI], F32, name="acc")
-                nc.tensor.matmul_mx(
-                    out=acc[:],
-                    lhsT=codes[:, cl * P:(cl + 1) * P].bitcast(E5M2X4),
-                    lhsT_scale=scales[:, cl * P:(cl + 1) * P],
-                    rhs=w_codes[l][:].bitcast(E4M3X4),
-                    rhs_scale=w_scales[l][:],
-                    start=True,
-                    stop=True,
-                )
-                if cl == 3:
+                for rep in range(2 if (cl % 2 == 1 and i1 - i0 == MI) else 1):
+                    nc.tensor.matmul_mx(
+                        out=acc[:],
+                        lhsT=codes[:, cl * P:(cl + 1) * P].bitcast(E5M2X4),
+                        lhsT_scale=scales[:, cl * P:(cl + 1) * P],
+                        rhs=w_codes[l][:].bitcast(E4M3X4),
+                        rhs_scale=w_scales[l][:],
+                        start=True,
+                        stop=True,
+                    )
+                if cl == 3 and q % 2 == 1:
                     nc.scalar.copy(out=y[:, cl, i0:i1], in_=acc[:, i0:i1])
                 else:
                     nc.vector.tensor_copy(out=y[:, cl, i0:i1], in_=acc[:, i0:i1])
@@ -165,9 +164,9 @@ def tile_irrepsstridelinear_t_kernel(tc, x, w0, w1, w2, w3, grad_out, out):
                 op1=ADD,
             )
             if cut < i1:
-                nc.vector.tensor_copy(out=z[:, cut:i1, 4 * q:4 * q + 4], in_=y[:, :, cut:i1].rearrange("p c i -> p i c"))
+                nc.scalar.copy(out=z[:, cut:i1, 4 * q:4 * q + 4], in_=y[:, :, cut:i1].rearrange("p c i -> p i c"))
 
-        units = [(nb, q) for nb in range(NB) for q in reversed(range(QUADS))]
+        units = [(nb, q) for nb in range(NB) for q in range(QUADS)]
         jobs = [(k, 0, MI) for k in range(len(units) - QUADS)]
         for r in range(2):
             jobs.extend([(k, r * MI // 2, (r + 1) * MI // 2) for k in range(len(units) - QUADS, len(units))])
@@ -188,31 +187,25 @@ def tile_irrepsstridelinear_t_kernel(tc, x, w0, w1, w2, w3, grad_out, out):
         def finish(j):
             k, i0, i1 = jobs[j]
             nb, q = units[k]
-            if k % QUADS == 0 and i0 == 0:
+            if q == 0 and i0 == 0:
                 z_of[nb] = zpool.tile([P, MI, C], F32, name="z")
             interleave(z_of[nb], planes[j], q, i0, i1)
-            if k % QUADS == QUADS - 1:
+            if q == QUADS - 1:
                 mid = (i0 + i1) // 2
                 store(nb, z_of[nb], i0, mid)
                 store(nb, z_of[nb], mid, i1)
 
-        def w_for(j):
-            if j < len(jobs):
-                q = units[jobs[j][0]][1]
-                for cl in range(4):
-                    w_prepare(degree(4 * q + cl))
-
         regroup(0)
-        w_for(0)
-        quantise(0)
         regroup(1)
+        quantise(0)
         quantise(1)
         for j in range(len(jobs)):
             k, i0, i1 = jobs[j]
+            for l in range(len(w_codes), degree(4 * units[k][1] + 3) + 1):
+                w_prepare(l)
             regroup(j + 2)
             planes[j] = multiply(units[k][1], ready[k][0], ready[k][1], i0, i1)
             quantise(j + 2)
-            w_for(j + 1)
             if j >= LAG:
                 finish(j - LAG)
         for j in range(len(jobs) - LAG, len(jobs)):

@@ -52,7 +52,7 @@ def tile_irrepsstridelinear_t_kernel(tc, x, w0, w1, w2, w3, grad_out, out):
         make_identity(nc, ident[:])
 
         g_sb = []
-        w_sb = []
+        w_sb = {}
 
         def load_g(nb):
             t = gpool.tile([P, MO * C], BF16, name="g_sb%d" % nb)
@@ -65,9 +65,9 @@ def tile_irrepsstridelinear_t_kernel(tc, x, w0, w1, w2, w3, grad_out, out):
                 )
 
         load_g(0)
-        for l in range(4):
+        for l in reversed(range(4)):
             t = wpool.tile([P, 4, MO], BF16, name="w_sb%d" % l)
-            w_sb.append(t)
+            w_sb[l] = t
             nc.sync.dma_start(out=t[:], in_=weights[l].rearrange("(b p) o -> p b o", p=P))
         for nb in range(1, NB):
             load_g(nb)
@@ -101,10 +101,12 @@ def tile_irrepsstridelinear_t_kernel(tc, x, w0, w1, w2, w3, grad_out, out):
             nc.vector.quantize_mx(out=codes[:].bitcast(E5M2X4), scales=scales[:], in_=grouped[:])
             return codes, scales
 
-        w_codes = []
-        w_scales = []
+        w_codes = {}
+        w_scales = {}
 
         def w_prepare(l):
+            if l in w_codes:
+                return
             words = w_sb[l][:].bitcast(F32)
             grouped = wstage.tile([P, MI * 4], BF16, name="w_grouped", align_bytes=64)
             gw = grouped[:].bitcast(F32)
@@ -123,8 +125,8 @@ def tile_irrepsstridelinear_t_kernel(tc, x, w0, w1, w2, w3, grad_out, out):
             codes = wpool.tile([P, MI], U32, name="w_codes%d" % l, align_bytes=64)
             scales = wpool.tile([P, MI], U8, name="w_scales%d" % l, align_bytes=64)
             nc.vector.quantize_mx(out=codes[:].bitcast(E4M3X4), scales=scales[:], in_=grouped[:])
-            w_codes.append(codes)
-            w_scales.append(scales)
+            w_codes[l] = codes
+            w_scales[l] = scales
 
         def store(nb, z, i0, i1):
             nc.sync.dma_start(
@@ -137,16 +139,15 @@ def tile_irrepsstridelinear_t_kernel(tc, x, w0, w1, w2, w3, grad_out, out):
             for cl in range(4):
                 l = degree(4 * q + cl)
                 acc = psum_o.tile([P, MI], F32, name="acc")
-                for rep in range(2 if (cl % 2 == 1 and i1 - i0 == MI) else 1):
-                    nc.tensor.matmul_mx(
-                        out=acc[:],
-                        lhsT=codes[:, cl * P:(cl + 1) * P].bitcast(E5M2X4),
-                        lhsT_scale=scales[:, cl * P:(cl + 1) * P],
-                        rhs=w_codes[l][:].bitcast(E4M3X4),
-                        rhs_scale=w_scales[l][:],
-                        start=True,
-                        stop=True,
-                    )
+                nc.tensor.matmul_mx(
+                    out=acc[:],
+                    lhsT=codes[:, cl * P:(cl + 1) * P].bitcast(E5M2X4),
+                    lhsT_scale=scales[:, cl * P:(cl + 1) * P],
+                    rhs=w_codes[l][:].bitcast(E4M3X4),
+                    rhs_scale=w_scales[l][:],
+                    start=True,
+                    stop=True,
+                )
                 if cl == 3 and q % 2 == 1:
                     nc.scalar.copy(out=y[:, cl, i0:i1], in_=acc[:, i0:i1])
                 else:
@@ -166,7 +167,7 @@ def tile_irrepsstridelinear_t_kernel(tc, x, w0, w1, w2, w3, grad_out, out):
             if cut < i1:
                 nc.scalar.copy(out=z[:, cut:i1, 4 * q:4 * q + 4], in_=y[:, :, cut:i1].rearrange("p c i -> p i c"))
 
-        units = [(nb, q) for nb in range(NB) for q in range(QUADS)]
+        units = [(nb, q) for nb in range(NB) for q in reversed(range(QUADS))]
         jobs = [(k, 0, MI) for k in range(len(units) - QUADS)]
         for r in range(2):
             jobs.extend([(k, r * MI // 2, (r + 1) * MI // 2) for k in range(len(units) - QUADS, len(units))])
@@ -187,25 +188,31 @@ def tile_irrepsstridelinear_t_kernel(tc, x, w0, w1, w2, w3, grad_out, out):
         def finish(j):
             k, i0, i1 = jobs[j]
             nb, q = units[k]
-            if q == 0 and i0 == 0:
+            if k % QUADS == 0 and i0 == 0:
                 z_of[nb] = zpool.tile([P, MI, C], F32, name="z")
             interleave(z_of[nb], planes[j], q, i0, i1)
-            if q == QUADS - 1:
+            if k % QUADS == QUADS - 1:
                 mid = (i0 + i1) // 2
                 store(nb, z_of[nb], i0, mid)
                 store(nb, z_of[nb], mid, i1)
 
+        def w_for(j):
+            if j < len(jobs):
+                q = units[jobs[j][0]][1]
+                for cl in range(4):
+                    w_prepare(degree(4 * q + cl))
+
         regroup(0)
-        regroup(1)
+        w_for(0)
         quantise(0)
+        regroup(1)
         quantise(1)
         for j in range(len(jobs)):
             k, i0, i1 = jobs[j]
-            for l in range(len(w_codes), degree(4 * units[k][1] + 3) + 1):
-                w_prepare(l)
             regroup(j + 2)
             planes[j] = multiply(units[k][1], ready[k][0], ready[k][1], i0, i1)
             quantise(j + 2)
+            w_for(j + 1)
             if j >= LAG:
                 finish(j - LAG)
         for j in range(len(jobs) - LAG, len(jobs)):

@@ -154,18 +154,19 @@ def tile_irrepsstridelinear_t_kernel(tc, x, w0, w1, w2, w3, grad_out, out):
                     nc.vector.tensor_copy(out=y[:, cl, i0:i1], in_=acc[:, i0:i1])
             return y
 
-        def interleave(z, y, q, i0, i1):
-            cut = i0 + (i1 - i0) * G_NUM // 8
-            nc.gpsimd.tensor_scalar(
-                out=z[:, i0:cut, 4 * q:4 * q + 4],
-                in0=y[:, :, i0:cut].rearrange("p c i -> p i c"),
-                scalar1=1.0,
-                scalar2=0.0,
-                op0=MULT,
-                op1=ADD,
-            )
-            if cut < i1:
-                nc.scalar.copy(out=z[:, cut:i1, 4 * q:4 * q + 4], in_=y[:, :, cut:i1].rearrange("p c i -> p i c"))
+        def interleave(z, y, q, i0, i1, cut):
+            g_end = max(i0, min(i1, cut))
+            if i0 < g_end:
+                nc.gpsimd.tensor_scalar(
+                    out=z[:, i0:g_end, 4 * q:4 * q + 4],
+                    in0=y[:, :, i0:g_end].rearrange("p c i -> p i c"),
+                    scalar1=1.0,
+                    scalar2=0.0,
+                    op0=MULT,
+                    op1=ADD,
+                )
+            if g_end < i1:
+                nc.scalar.copy(out=z[:, g_end:i1, 4 * q:4 * q + 4], in_=y[:, :, g_end:i1].rearrange("p c i -> p i c"))
 
         units = [(nb, q) for nb in range(NB) for q in reversed(range(QUADS))]
         jobs = [(k, 0, MI) for k in range(len(units) - QUADS)]
@@ -190,11 +191,15 @@ def tile_irrepsstridelinear_t_kernel(tc, x, w0, w1, w2, w3, grad_out, out):
             nb, q = units[k]
             if k % QUADS == 0 and i0 == 0:
                 z_of[nb] = zpool.tile([P, MI, C], F32, name="z")
-            interleave(z_of[nb], planes[j], q, i0, i1)
+            cut = i0 + (i1 - i0) * G_NUM // 8
             if k % QUADS == QUADS - 1:
                 mid = (i0 + i1) // 2
+                interleave(z_of[nb], planes[j], q, i0, mid, cut)
                 store(nb, z_of[nb], i0, mid)
+                interleave(z_of[nb], planes[j], q, mid, i1, cut)
                 store(nb, z_of[nb], mid, i1)
+            else:
+                interleave(z_of[nb], planes[j], q, i0, i1, cut)
 
         def w_for(j):
             if j < len(jobs):

from contextlib import ExitStack

import concourse.mybir as mybir
from concourse.masks import make_identity

F32 = mybir.dt.float32
BF16 = mybir.dt.bfloat16
U32 = mybir.dt.uint32
U8 = mybir.dt.uint8
E4M3X4 = mybir.dt.float8_e4m3fn_x4
E5M2X4 = mybir.dt.float8_e5m2_x4
MULT = mybir.AluOpType.mult
ADD = mybir.AluOpType.add

P = 128
N = 512
MI = 512
MO = 512
C = 16
NB = N // P
QUADS = C // 4
PINNED = True
LAG = 1
G_NUM = 6

FLOPS = 2 * N * MI * MO * C
BYTES = N * MO * C * 2 + 4 * MI * MO * 2 + N * MI * C * 4


def degree(c):
    return 0 if c < 1 else 1 if c < 4 else 2 if c < 9 else 3


def tile_irrepsstridelinear_t_kernel(tc, x, w0, w1, w2, w3, grad_out, out):
    nc = tc.nc
    weights = [w0, w1, w2, w3]
    with ExitStack() as ctx:
        const = ctx.enter_context(tc.tile_pool(name="const", bufs=1))
        gpool = ctx.enter_context(tc.tile_pool(name="gpool", bufs=1))
        wpool = ctx.enter_context(tc.tile_pool(name="wpool", bufs=1))
        wstage = ctx.enter_context(tc.tile_pool(name="wstage", bufs=2))
        grp = ctx.enter_context(tc.tile_pool(name="grp", bufs=3))
        qpool = ctx.enter_context(tc.tile_pool(name="qpool", bufs=6))
        ypool = ctx.enter_context(tc.tile_pool(name="ypool", bufs=4))
        zpool = ctx.enter_context(tc.tile_pool(name="zpool", bufs=2))
        psum_t = ctx.enter_context(tc.psum_pool(name="psum_t", bufs=4))
        psum_o = ctx.enter_context(tc.psum_pool(name="psum_o", bufs=4))
        if PINNED:
            ctx.enter_context(tc.manual_schedule())

        ident = const.tile([P, P], F32, name="ident")
        make_identity(nc, ident[:])

        g_sb = []
        w_sb = {}

        def load_g(nb):
            t = gpool.tile([P, MO * C], BF16, name="g_sb%d" % nb)
            g_sb.append(t)
            half = MO // 2
            for u in range(2):
                nc.sync.dma_start(
                    out=t[:, u * half * C:(u + 1) * half * C],
                    in_=grad_out[nb * P:(nb + 1) * P, u * half:(u + 1) * half, :].rearrange("n o c -> n (o c)"),
                )

        load_g(0)
        for l in reversed(range(4)):
            t = wpool.tile([P, 4, MO], BF16, name="w_sb%d" % l)
            w_sb[l] = t
            nc.sync.dma_start(out=t[:], in_=weights[l].rearrange("(b p) o -> p b o", p=P))
        for nb in range(1, NB):
            load_g(nb)

        def g_transposes(nb, q):
            words = g_sb[nb][:].bitcast(F32).rearrange("p (u j e c) -> p u e c j", u=2, j=P, e=2, c=C // 2)
            banks = []
            for cpl in range(2):
                bank = psum_t.tile([P, 4 * P], F32, name="tbank")
                for u in range(2):
                    for e in range(2):
                        t = 2 * u + e
                        nc.tensor.transpose(bank[:, t * P:(t + 1) * P], words[:, u, e, 2 * q + cpl, :], ident[:])
                banks.append(bank)
            return banks

        def g_regroup(banks, vector_helps):
            grouped = grp.tile([P, 4 * P * 4], BF16, name="grouped", align_bytes=64)
            for cpl in range(2):
                dst = grouped[:, cpl * 1024:(cpl + 1) * 1024].rearrange("p (e n t) -> p e n t", e=2, n=P, t=4)
                src = banks[cpl][:].bitcast(BF16).rearrange("p (t n e) -> p e n t", t=4, n=P, e=2)
                if vector_helps and cpl == 1:
                    nc.vector.tensor_copy(out=dst, in_=src)
                else:
                    nc.scalar.copy(out=dst, in_=src)
            return grouped

        def g_quantise(grouped):
            codes = qpool.tile([P, 4 * P], U32, name="g_codes", align_bytes=64)
            scales = qpool.tile([P, 4 * P], U8, name="g_scales", align_bytes=64)
            nc.vector.quantize_mx(out=codes[:].bitcast(E5M2X4), scales=scales[:], in_=grouped[:])
            return codes, scales

        w_codes = {}
        w_scales = {}

        def w_prepare(l):
            if l in w_codes:
                return
            words = w_sb[l][:].bitcast(F32)
            grouped = wstage.tile([P, MI * 4], BF16, name="w_grouped", align_bytes=64)
            gw = grouped[:].bitcast(F32)
            for bp in range(2):
                bank = psum_t.tile([P, 4 * P], F32, name="tbank")
                for bb in range(2):
                    for u in range(2):
                        s = 2 * bb + u
                        nc.tensor.transpose(bank[:, s * P:(s + 1) * P], words[:, 2 * bp + bb, u * P:(u + 1) * P], ident[:])
                dst = gw[:, bp * 512:(bp + 1) * 512].rearrange("p (b i u) -> p b i u", b=2, i=P, u=2)
                src = bank[:].rearrange("p (b u i) -> p b i u", b=2, u=2, i=P)
                if bp == 0:
                    nc.vector.tensor_copy(out=dst, in_=src)
                else:
                    nc.scalar.copy(out=dst, in_=src)
            codes = wpool.tile([P, MI], U32, name="w_codes%d" % l, align_bytes=64)
            scales = wpool.tile([P, MI], U8, name="w_scales%d" % l, align_bytes=64)
            nc.vector.quantize_mx(out=codes[:].bitcast(E4M3X4), scales=scales[:], in_=grouped[:])
            w_codes[l] = codes
            w_scales[l] = scales

        def store(nb, z, i0, i1):
            nc.sync.dma_start(
                out=out[nb * P:(nb + 1) * P, i0:i1, :].rearrange("n i c -> n (i c)"),
                in_=z[:, i0:i1, :].rearrange("p i c -> p (i c)"),
            )

        def multiply(q, codes, scales, i0, i1):
            y = ypool.tile([P, 4, MI], F32, name="y")
            for cl in range(4):
                l = degree(4 * q + cl)
                acc = psum_o.tile([P, MI], F32, name="acc")
                nc.tensor.matmul_mx(
                    out=acc[:],
                    lhsT=codes[:, cl * P:(cl + 1) * P].bitcast(E5M2X4),
                    lhsT_scale=scales[:, cl * P:(cl + 1) * P],
                    rhs=w_codes[l][:].bitcast(E4M3X4),
                    rhs_scale=w_scales[l][:],
                    start=True,
                    stop=True,
                )
                if cl == 3 and q % 2 == 1:
                    nc.scalar.copy(out=y[:, cl, i0:i1], in_=acc[:, i0:i1])
                else:
                    nc.vector.tensor_copy(out=y[:, cl, i0:i1], in_=acc[:, i0:i1])
            return y

        def interleave(z, y, q, i0, i1, cut):
            g_end = max(i0, min(i1, cut))
            if i0 < g_end:
                nc.gpsimd.tensor_scalar(
                    out=z[:, i0:g_end, 4 * q:4 * q + 4],
                    in0=y[:, :, i0:g_end].rearrange("p c i -> p i c"),
                    scalar1=1.0,
                    scalar2=0.0,
                    op0=MULT,
                    op1=ADD,
                )
            if g_end < i1:
                nc.scalar.copy(out=z[:, g_end:i1, 4 * q:4 * q + 4], in_=y[:, :, g_end:i1].rearrange("p c i -> p i c"))

        units = [(nb, q) for nb in range(NB) for q in reversed(range(QUADS))]
        jobs = [(k, 0, MI) for k in range(len(units) - QUADS)]
        for r in range(2):
            jobs.extend([(k, r * MI // 2, (r + 1) * MI // 2) for k in range(len(units) - QUADS, len(units))])
        ready = {}
        staged = {}
        planes = {}
        z_of = {}

        def regroup(k):
            if k < len(units):
                nb, q = units[k]
                staged[k] = g_regroup(g_transposes(nb, q), k < 2)

        def quantise(k):
            if k < len(units):
                ready[k] = g_quantise(staged[k])

        def finish(j):
            k, i0, i1 = jobs[j]
            nb, q = units[k]
            if k % QUADS == 0 and i0 == 0:
                z_of[nb] = zpool.tile([P, MI, C], F32, name="z")
            cut = i0 + (i1 - i0) * G_NUM // 8
            if k % QUADS == QUADS - 1:
                mid = (i0 + i1) // 2
                interleave(z_of[nb], planes[j], q, i0, mid, cut)
                store(nb, z_of[nb], i0, mid)
                interleave(z_of[nb], planes[j], q, mid, i1, cut)
                store(nb, z_of[nb], mid, i1)
            else:
                interleave(z_of[nb], planes[j], q, i0, i1, cut)

        def w_for(j):
            if j < len(jobs):
                q = units[jobs[j][0]][1]
                for cl in range(4):
                    w_prepare(degree(4 * q + cl))

        regroup(0)
        w_for(0)
        quantise(0)
        regroup(1)
        quantise(1)
        for j in range(len(jobs)):
            k, i0, i1 = jobs[j]
            regroup(j + 2)
            planes[j] = multiply(units[k][1], ready[k][0], ready[k][1], i0, i1)
            quantise(j + 2)
            w_for(j + 1)
            if j >= LAG:
                finish(j - LAG)
        for j in range(len(jobs) - LAG, len(jobs)):
            finish(j)
